import numpy as np
import ml_dtypes


BF16 = ml_dtypes.bfloat16


def bf(x):
    return np.asarray(x, np.float32).astype(BF16)


def f64(x):
    return np.asarray(x).astype(np.float64)


E2M1 = np.array([0.0, 0.5, 1.0, 1.5, 2.0, 3.0, 4.0, 6.0, -0.0, -0.5, -1.0, -1.5, -2.0, -3.0, -4.0, -6.0])


def pack_weight(w, fmt):
    k, n = w.shape
    w = f64(bf(w)).reshape(k // 32, 32, n)
    amax = np.abs(w).max(1)
    if fmt == "e4m3":
        byte = np.frexp(amax)[1] - 1 + 127 - 7
    else:
        mant, ex = np.frexp(amax / 6.0)
        byte = np.where(mant > 0.5, ex, ex - 1) + 127
    byte = np.clip(np.where(amax > 0, byte, 1), 1, 254)
    scaled = (w * np.exp2(127.0 - byte)[:, None, :]).reshape(k, n).astype(np.float32)
    by_word = np.ascontiguousarray(scaled.reshape(k // 512, 128, 4, n).transpose(0, 1, 3, 2))
    if fmt == "e4m3":
        words = by_word.astype(ml_dtypes.float8_e4m3fn).view(np.uint8)
    else:
        c = by_word.astype(ml_dtypes.float4_e2m1fn).view(np.uint8) & 0xF
        words = c[..., 0::2] | (c[..., 1::2] << 4)
    return np.ascontiguousarray(words), np.ascontiguousarray(byte.astype(np.uint8).reshape(k // 512, 16, n))


def unpack_weight(words, scales, fmt):
    g, p, n, _ = words.shape
    if fmt == "e4m3":
        vals = np.ascontiguousarray(words).view(ml_dtypes.float8_e4m3fn).astype(np.float64)
    else:
        nib = np.empty((g, p, n, 4), np.uint8)
        nib[..., 0::2] = words & 0xF
        nib[..., 1::2] = words >> 4
        vals = E2M1[nib]
    vals = vals * np.repeat(np.exp2(scales.astype(np.float64) - 127.0), 8, axis=1)[..., None]
    return vals.transpose(0, 1, 3, 2).reshape(g * 512, n)

def pack4(w):
    words, scales = pack_weight(w, "e2m1")
    return words.reshape(words.shape[0], 128, -1), scales


def unpack4(words, scales):
    return unpack_weight(words.reshape(words.shape[0], 128, -1, 2), scales, "e2m1")


def kspread(k):
    return np.exp2(np.repeat(np.random.randint(-6, 7, k // 32), 32).astype(np.float64))


B, T, E, H, HKV, HD, SB = 1, 1024, 4096, 16, 8, 128, 512
THETA = 10000.0


def rotate_half(u):
    u1, u2 = np.split(u, 2, axis=-1)
    return np.concatenate([-u2, u1], axis=-1)


def xpos_tables(seqlen):
    half_idx = f64(np.arange(0, HD, 2))
    inv_freq = 1.0 / (THETA ** (half_idx / HD))
    t = f64(np.arange(seqlen))
    freqs = t[:, None] * inv_freq[None, :]
    emb = np.concatenate([freqs, freqs], axis=-1)
    scale_vec = (half_idx + 0.4 * HD) / (1.4 * HD)
    power = (t - seqlen // 2) / SB
    scale = scale_vec[None, :] ** power[:, None]
    scale = np.concatenate([scale, scale], axis=-1)
    return np.cos(emb), np.sin(emb), scale


def setup_inputs():
    s = kspread(E)
    w = 1.0 / np.sqrt(E)
    x = np.random.standard_normal((B, T, E)) * s
    x_words, x_scales = pack4(np.ascontiguousarray(x.reshape(B * T, E).T))
    q_words, q_scales = pack4(np.random.standard_normal((E, H * HD)) * w / s[:, None])
    k_words, k_scales = pack4(np.random.standard_normal((E, HKV * HD)) * w / s[:, None])
    v_words, v_scales = pack4(np.random.standard_normal((E, HKV * HD)) * w / s[:, None])
    return {"x_words": x_words, "x_scales": x_scales,
            "W_q_words": q_words, "W_q_scales": q_scales,
            "W_k_words": k_words, "W_k_scales": k_scales,
            "W_v_words": v_words, "W_v_scales": v_scales}


def reference(x_words, x_scales, W_q_words, W_q_scales, W_k_words, W_k_scales, W_v_words, W_v_scales):
    xq = unpack4(x_words, x_scales).T.reshape(B, T, E)
    q = (xq @ unpack4(W_q_words, W_q_scales)).reshape(B, T, H, HD)
    k = (xq @ unpack4(W_k_words, W_k_scales)).reshape(B, T, HKV, HD)
    v = (xq @ unpack4(W_v_words, W_v_scales)).reshape(B, T, HKV, HD)
    cos, sin, scale = xpos_tables(T)
    cos = cos[None, :, None, :]
    sin = sin[None, :, None, :]
    scale = scale[None, :, None, :]
    q = q * scale
    q = q * cos + rotate_half(q) * sin
    k = k / scale
    k = k * cos + rotate_half(k) * sin
    return q, k, v

@@ -1,0 +1,268 @@
+from contextlib import ExitStack
+
+import concourse.mybir as mybir
+
+T, E, HD = 1024, 4096, 128
+FLOPS = 2 * T * E * 4096
+
+F32 = mybir.dt.float32
+I32 = mybir.dt.int32
+BF16 = mybir.dt.bfloat16
+U8 = mybir.dt.uint8
+FP4X4 = mybir.dt.float4_e2m1fn_x4
+ALU = mybir.AluOpType
+ACT = mybir.ActivationFunctionType
+
+P = 128
+PASSES = E // 512
+TOK_TILES = T // P
+NB = 512
+HEADS = NB // HD
+HALF = HD // 2
+TWO_PI = 6.283185307179586
+WARM_FREE = 4
+WARM_HELD = 6
+
+
+def load_codes(nc, tile, words, g0, g1, c0, c1):
+    nc.sync.dma_start(
+        out=tile[:].bitcast(I32),
+        in_=words[g0:g1, :, 2 * c0 : 2 * c1].rearrange("g p n -> p g n").bitcast(I32),
+    )
+
+
+def load_scales(nc, tile, scales, g0, g1, c0, c1):
+    for r in range(4):
+        nc.sync.dma_start(
+            out=tile[r : P : 32, :, :].bitcast(I32),
+            in_=scales[g0:g1, r : 16 : 4, c0:c1].rearrange("g q n -> q g n").bitcast(I32),
+        )
+
+
+def tile_multiheadselfattention_pa_kernel(
+    tc, x_words, x_scales, wq_words, wq_scales, wk_words, wk_scales, wv_words, wv_scales, out_q, out_k, out_v
+):
+    nc = tc.nc
+    outs = {
+        "q": out_q.rearrange("b t h d -> (b t) (h d)"),
+        "k": out_k.rearrange("b t h d -> (b t) (h d)"),
+        "v": out_v.rearrange("b t h d -> (b t) (h d)"),
+    }
+    weights = {"q": (wq_words, wq_scales), "k": (wk_words, wk_scales), "v": (wv_words, wv_scales)}
+    blocks = [("v", 0), ("q", 0), ("q", 1), ("q", 2), ("q", 3), ("k", 0), ("k", 1), ("v", 1)]
+    code_runs = [(0, 1), (1, 4), (4, 8)]
+    scale_runs = [(0, 2), (2, 8)]
+
+    with ExitStack() as ctx:
+        ctx.enter_context(tc.manual_schedule())
+        keep = ctx.enter_context(tc.tile_pool(name="keep", bufs=1))
+        stage = ctx.enter_context(tc.tile_pool(name="stage", bufs=1))
+        psum = ctx.enter_context(tc.psum_pool(name="psum", bufs=8))
+
+        warm = keep.tile([P, NB], BF16, name="warm")
+        nc.gpsimd.memset(warm[:], 0.0)
+
+        pos_i = keep.tile([P, TOK_TILES], I32, name="pos_i")
+        nc.gpsimd.iota(pos_i[:], pattern=[[P, TOK_TILES]], base=0, channel_multiplier=1)
+        idx_i = keep.tile([P, HALF], I32, name="idx_i")
+        nc.gpsimd.iota(idx_i[:], pattern=[[1, HALF]], base=0, channel_multiplier=0)
+
+        x_code, x_scale = [], []
+        w_code = [[] for b in blocks]
+        w_scale = [[] for b in blocks]
+
+        xc_tiles, wc_tiles, xs_tiles, ws_tiles = [], [], [], []
+        for r, (g0, g1) in enumerate(code_runs):
+            xc = keep.tile([P, g1 - g0, 2 * T], U8, name="xc%d" % r, align_bytes=64)
+            wc = keep.tile([P, g1 - g0, 2 * NB], U8, name="wc0_%d" % r, align_bytes=64)
+            xc_tiles.append(xc)
+            wc_tiles.append(wc)
+            for g in range(g0, g1):
+                x_code.append((xc, g - g0))
+                w_code[0].append((wc, g - g0))
+        for r, (g0, g1) in enumerate(scale_runs):
+            xs = keep.tile([P, g1 - g0, T], U8, name="xs%d" % r, align_bytes=64)
+            ws = keep.tile([P, g1 - g0, NB], U8, name="ws0_%d" % r, align_bytes=64)
+            xs_tiles.append(xs)
+            ws_tiles.append(ws)
+            for g in range(g0, g1):
+                x_scale.append((xs, g - g0))
+                w_scale[0].append((ws, g - g0))
+
+        kind0, col0 = blocks[0]
+        w0_words, w0_scales = weights[kind0]
+        c0, c1 = col0 * NB, (col0 + 1) * NB
+
+        nc.vector.memset(xs_tiles[0][:].bitcast(I32), 0)
+        nc.vector.memset(ws_tiles[0][:].bitcast(I32), 0)
+        warm_acc = psum.tile([P, NB], F32, name="acc")
+        for i in range(WARM_FREE):
+            nc.tensor.matmul(out=warm_acc[:], lhsT=warm[:, 0:P], rhs=warm[:], start=True, stop=True)
+        load_codes(nc, xc_tiles[0], x_words, 0, 1, 0, T)
+        load_codes(nc, wc_tiles[0], w0_words, 0, 1, c0, c1)
+        gate = keep.tile([P, 4], U8, name="gate")
+        nc.gpsimd.tensor_copy(out=gate[:], in_=wc_tiles[0][:, 0, 0:4])
+        held = keep.tile([P, P], BF16, name="held")
+        nc.gpsimd.memset(held[:], 0.0)
+        for i in range(WARM_HELD):
+            nc.tensor.matmul(out=warm_acc[:], lhsT=held[:], rhs=warm[:], start=True, stop=True)
+        load_scales(nc, xs_tiles[0], x_scales, 0, 2, 0, T)
+        load_scales(nc, ws_tiles[0], w0_scales, 0, 2, c0, c1)
+        nc.vector.memset(xs_tiles[1][:].bitcast(I32), 0)
+        nc.vector.memset(ws_tiles[1][:].bitcast(I32), 0)
+        load_codes(nc, xc_tiles[1], x_words, 1, 4, 0, T)
+        load_codes(nc, wc_tiles[1], w0_words, 1, 4, c0, c1)
+        load_scales(nc, xs_tiles[1], x_scales, 2, 8, 0, T)
+        load_scales(nc, ws_tiles[1], w0_scales, 2, 8, c0, c1)
+        load_codes(nc, xc_tiles[2], x_words, 4, 8, 0, T)
+        load_codes(nc, wc_tiles[2], w0_words, 4, 8, c0, c1)
+
+        late_planes = []
+        for b in range(1, len(blocks)):
+            wc = keep.tile([P, PASSES, 2 * NB], U8, name="wc%d" % b, align_bytes=64)
+            ws = keep.tile([P, PASSES, NB], U8, name="ws%d" % b, align_bytes=64)
+            late_planes.append((b, wc, ws))
+            for g in range(PASSES):
+                w_code[b].append((wc, g))
+                w_scale[b].append((ws, g))
+
+        def load_block(b, wc, ws):
+            kind, col = blocks[b]
+            words, scales = weights[kind]
+            nc.vector.memset(ws[:].bitcast(I32), 0)
+            load_codes(nc, wc, words, 0, PASSES, col * NB, (col + 1) * NB)
+            load_scales(nc, ws, scales, 0, PASSES, col * NB, (col + 1) * NB)
+
+        for b, wc, ws in late_planes[:2]:
+            load_block(b, wc, ws)
+
+        posf = keep.tile([P, TOK_TILES], F32, name="posf")
+        nc.vector.tensor_copy(out=posf[:], in_=pos_i[:])
+        idxf = keep.tile([P, HALF], F32, name="idxf")
+        nc.vector.tensor_copy(out=idxf[:], in_=idx_i[:])
+        base = keep.tile([P, HALF], F32, name="base")
+        nc.vector.tensor_scalar(
+            out=base[:], in0=idxf[:], scalar1=2.0 / (1.4 * HD), scalar2=0.4 / 1.4, op0=ALU.mult, op1=ALU.add
+        )
+        lnb = keep.tile([P, HALF], F32, name="lnb")
+        nc.scalar.activation(out=lnb[:], in_=base[:], func=ACT.Ln)
+        power = keep.tile([P, TOK_TILES], F32, name="power")
+        nc.vector.tensor_scalar(
+            out=power[:], in0=posf[:], scalar1=-512.0, scalar2=1.0 / 512.0, op0=ALU.add, op1=ALU.mult
+        )
+        turns = keep.tile([P, HALF], F32, name="turns")
+        nc.vector.tensor_scalar(
+            out=turns[:, 0:1], in0=posf[:, 0:1], scalar1=0.0, scalar2=1.0 / TWO_PI, op0=ALU.mult, op1=ALU.add
+        )
+        n = 1
+        while n < HALF:
+            nc.vector.tensor_scalar(
+                out=turns[:, n : 2 * n], in0=turns[:, 0:n], scalar1=10000.0 ** (-n / float(HALF)), scalar2=None, op0=ALU.mult
+            )
+            n *= 2
+        shape3 = [P, TOK_TILES, HALF]
+        ang = keep.tile([P, TOK_TILES, 2, HALF], F32, name="ang")
+        nc.vector.tensor_tensor(
+            out=ang[:, :, 0, :],
+            in0=turns[:].unsqueeze(1).to_broadcast(shape3),
+            in1=posf[:].unsqueeze(2).to_broadcast(shape3),
+            op=ALU.mult,
+        )
+        expo = keep.tile(shape3, F32, name="expo")
+        nc.vector.tensor_tensor(
+            out=expo[:],
+            in0=lnb[:].unsqueeze(1).to_broadcast(shape3),
+            in1=power[:].unsqueeze(2).to_broadcast(shape3),
+            op=ALU.mult,
+        )
+        decay = keep.tile([P, 2, TOK_TILES, HALF], F32, name="decay")
+        nc.scalar.activation(out=decay[:, 0], in_=expo[:], func=ACT.Exp)
+        nc.scalar.activation(out=decay[:, 1], in_=expo[:], func=ACT.Exp, scale=-1.0)
+        nc.vector.tensor_scalar(out=ang[:, :, 1, :], in0=ang[:, :, 0, :], scalar1=0.25, scalar2=None, op0=ALU.add)
+        whole = keep.tile([P, TOK_TILES, 2, HALF], I32, name="whole")
+        nc.vector.tensor_copy(out=whole[:], in_=ang[:])
+        nc.vector.tensor_tensor(out=ang[:], in0=ang[:], in1=whole[:], op=ALU.subtract)
+        nc.vector.scalar_tensor_tensor(out=ang[:], in0=ang[:], scalar=0.5, in1=ang[:], op0=ALU.is_gt, op1=ALU.subtract)
+        sincos = keep.tile([P, TOK_TILES, 2, HALF], F32, name="sincos")
+        nc.scalar.activation(out=sincos[:], in_=ang[:], func=ACT.Sin, scale=-TWO_PI)
+
+        cos_tab, sin_tab = {}, {}
+        for j, kind in enumerate(("q", "k")):
+            ct = keep.tile([P, TOK_TILES, 2, HALF], F32, name="cos_" + kind)
+            st = keep.tile([P, TOK_TILES, 2, HALF], F32, name="sin_" + kind)
+            for two in range(2):
+                nc.vector.tensor_tensor(out=ct[:, :, two, :], in0=sincos[:, :, 1, :], in1=decay[:, j], op=ALU.mult)
+            nc.vector.tensor_tensor(out=st[:, :, 0, :], in0=sincos[:, :, 0, :], in1=decay[:, j], op=ALU.mult)
+            nc.vector.scalar_tensor_tensor(
+                out=st[:, :, 1, :], in0=sincos[:, :, 0, :], scalar=-1.0, in1=decay[:, j], op0=ALU.mult, op1=ALU.mult
+            )
+            cos_tab[kind] = ct
+            sin_tab[kind] = st
+
+        for b, wc, ws in late_planes[2:]:
+            load_block(b, wc, ws)
+
+        def mx_pass(acc, b, t, g, n0=0, n1=NB):
+            xc, xi = x_code[g]
+            xs, si = x_scale[g]
+            wc, wi = w_code[b][g]
+            ws, wj = w_scale[b][g]
+            nc.tensor.matmul_mx(
+                out=acc[:],
+                lhsT=xc[:, xi, 2 * P * t : 2 * P * (t + 1)].bitcast(FP4X4),
+                lhsT_scale=xs[:, si, P * t : P * (t + 1)],
+                rhs=wc[:, wi, 2 * n0 : 2 * n1].bitcast(FP4X4),
+                rhs_scale=ws[:, wj, n0:n1],
+                start=(g == 0),
+                stop=(g == PASSES - 1),
+            )
+
+        def finish(acc, b, t, n0=0, n1=NB):
+            kind, col = blocks[b]
+            dst = outs[kind][P * t : P * (t + 1), col * NB + n0 : col * NB + n1]
+            if kind == "v":
+                vo = stage.tile([P, n1 - n0], F32, name="vo", bufs=10)
+                nc.scalar.copy(out=vo[:], in_=acc[:])
+                nc.sync.dma_start(out=dst, in_=vo[:])
+                return
+            shape_h = [P, HEADS, HD]
+            acc_h = acc[:].rearrange("p (h d) -> p h d", h=HEADS)
+            direct = stage.tile([P, HEADS, 2, HALF], F32, name="direct", bufs=6)
+            cross = stage.tile([P, HEADS, 2, HALF], F32, name="cross", bufs=4)
+            nc.vector.tensor_tensor(
+                out=direct[:].rearrange("p h two i -> p h (two i)"),
+                in0=acc_h,
+                in1=cos_tab[kind][:, t].rearrange("p two i -> p (two i)").unsqueeze(1).to_broadcast(shape_h),
+                op=ALU.mult,
+            )
+            nc.vector.tensor_tensor(
+                out=cross[:].rearrange("p h two i -> p h (two i)"),
+                in0=acc_h,
+                in1=sin_tab[kind][:, t].rearrange("p two i -> p (two i)").unsqueeze(1).to_broadcast(shape_h),
+                op=ALU.mult,
+            )
+            for two in range(2):
+                nc.vector.tensor_tensor(
+                    out=direct[:, :, two, :], in0=direct[:, :, two, :], in1=cross[:, :, 1 - two, :], op=ALU.add
+                )
+            nc.sync.dma_start(out=dst, in_=direct[:].rearrange("p h two i -> p (h two i)"))
+
+        accs = []
+        for t in range(TOK_TILES):
+            acc0 = psum.tile([P, NB], F32, name="acc")
+            accs.append(acc0)
+        for g in range(PASSES):
+            for t in range(TOK_TILES):
+                mx_pass(accs[t], 0, t, g)
+        for t in range(TOK_TILES):
+            finish(accs[t], 0, t)
+
+        last = (len(blocks) - 1, TOK_TILES - 1)
+        for b in range(1, len(blocks)):
+            for t in range(TOK_TILES):
+                cuts = [0, NB // 2, NB] if (b, t) == last else [0, NB]
+                for n0, n1 in zip(cuts[:-1], cuts[1:]):
+                    acc = psum.tile([P, n1 - n0], F32, name="acc")
+                    for g in range(PASSES):
+                        mx_pass(acc, b, t, g, n0, n1)
+                    finish(acc, b, t, n0, n1)

@@ -73,16 +73,16 @@ def tile_multiheadselfattention_pa_kernel(
 
         xc_tiles, wc_tiles, xs_tiles, ws_tiles = [], [], [], []
         for r, (g0, g1) in enumerate(code_runs):
-            xc = keep.tile([P, g1 - g0, 2 * T], U8, name="xc%d" % r, align_bytes=64)
-            wc = keep.tile([P, g1 - g0, 2 * NB], U8, name="wc0_%d" % r, align_bytes=64)
+            xc = keep.tile([P, g1 - g0, 2 * T], U8, name="xc%d" % r, align_bytes=256)
+            wc = keep.tile([P, g1 - g0, 2 * NB], U8, name="wc0_%d" % r, align_bytes=256)
             xc_tiles.append(xc)
             wc_tiles.append(wc)
             for g in range(g0, g1):
                 x_code.append((xc, g - g0))
                 w_code[0].append((wc, g - g0))
         for r, (g0, g1) in enumerate(scale_runs):
-            xs = keep.tile([P, g1 - g0, T], U8, name="xs%d" % r, align_bytes=64)
-            ws = keep.tile([P, g1 - g0, NB], U8, name="ws0_%d" % r, align_bytes=64)
+            xs = keep.tile([P, g1 - g0, T], U8, name="xs%d" % r, align_bytes=256)
+            ws = keep.tile([P, g1 - g0, NB], U8, name="ws0_%d" % r, align_bytes=256)
             xs_tiles.append(xs)
             ws_tiles.append(ws)
             for g in range(g0, g1):
@@ -119,8 +119,8 @@ def tile_multiheadselfattention_pa_kernel(
 
         late_planes = []
         for b in range(1, len(blocks)):
-            wc = keep.tile([P, PASSES, 2 * NB], U8, name="wc%d" % b, align_bytes=64)
-            ws = keep.tile([P, PASSES, NB], U8, name="ws%d" % b, align_bytes=64)
+            wc = keep.tile([P, PASSES, 2 * NB], U8, name="wc%d" % b, align_bytes=256)
+            ws = keep.tile([P, PASSES, NB], U8, name="ws%d" % b, align_bytes=256)
             late_planes.append((b, wc, ws))
             for g in range(PASSES):
                 w_code[b].append((wc, g))

@@ -31,8 +31,8 @@ def load_codes(nc, tile, words, g0, g1, c0, c1):
     )
 
 
-def load_scales(nc, tile, scales, g0, g1, c0, c1):
-    for r in range(4):
+def load_scales(nc, tile, scales, g0, g1, c0, c1, rows=(0, 1, 2, 3)):
+    for r in rows:
         nc.sync.dma_start(
             out=tile[r : P : 32, :, :].bitcast(I32),
             in_=scales[g0:g1, r : 16 : 4, c0:c1].rearrange("g q n -> q g n").bitcast(I32),
@@ -51,7 +51,8 @@ def tile_multiheadselfattention_pa_kernel(
     weights = {"q": (wq_words, wq_scales), "k": (wk_words, wk_scales), "v": (wv_words, wv_scales)}
     blocks = [("v", 0), ("q", 0), ("q", 1), ("q", 2), ("q", 3), ("k", 0), ("k", 1), ("v", 1)]
     code_runs = [(0, 1), (1, 4), (4, 8)]
-    scale_runs = [(0, 2), (2, 8)]
+    x_scale_runs = [(0, 2), (2, 8)]
+    w_scale_runs = [(0, 8)]
 
     with ExitStack() as ctx:
         ctx.enter_context(tc.manual_schedule())
@@ -80,13 +81,15 @@ def tile_multiheadselfattention_pa_kernel(
             for g in range(g0, g1):
                 x_code.append((xc, g - g0))
                 w_code[0].append((wc, g - g0))
-        for r, (g0, g1) in enumerate(scale_runs):
+        for r, (g0, g1) in enumerate(x_scale_runs):
             xs = keep.tile([P, g1 - g0, T], U8, name="xs%d" % r, align_bytes=256)
-            ws = keep.tile([P, g1 - g0, NB], U8, name="ws0_%d" % r, align_bytes=256)
             xs_tiles.append(xs)
-            ws_tiles.append(ws)
             for g in range(g0, g1):
                 x_scale.append((xs, g - g0))
+        for r, (g0, g1) in enumerate(w_scale_runs):
+            ws = keep.tile([P, g1 - g0, NB], U8, name="ws0_%d" % r, align_bytes=256)
+            ws_tiles.append(ws)
+            for g in range(g0, g1):
                 w_scale[0].append((ws, g - g0))
 
         kind0, col0 = blocks[0]
@@ -106,14 +109,13 @@ def tile_multiheadselfattention_pa_kernel(
         nc.gpsimd.memset(held[:], 0.0)
         for i in range(WARM_HELD):
             nc.tensor.matmul(out=warm_acc[:], lhsT=held[:], rhs=warm[:], start=True, stop=True)
-        load_scales(nc, xs_tiles[0], x_scales, 0, 2, 0, T)
-        load_scales(nc, ws_tiles[0], w0_scales, 0, 2, c0, c1)
+        load_scales(nc, xs_tiles[0], x_scales, 0, 2, 0, T, rows=(0, 1))
+        load_scales(nc, ws_tiles[0], w0_scales, 0, 8, c0, c1)
+        load_scales(nc, xs_tiles[0], x_scales, 0, 2, 0, T, rows=(2, 3))
         nc.vector.memset(xs_tiles[1][:].bitcast(I32), 0)
-        nc.vector.memset(ws_tiles[1][:].bitcast(I32), 0)
         load_codes(nc, xc_tiles[1], x_words, 1, 4, 0, T)
         load_codes(nc, wc_tiles[1], w0_words, 1, 4, c0, c1)
         load_scales(nc, xs_tiles[1], x_scales, 2, 8, 0, T)
-        load_scales(nc, ws_tiles[1], w0_scales, 2, 8, c0, c1)
         load_codes(nc, xc_tiles[2], x_words, 4, 8, 0, T)
         load_codes(nc, wc_tiles[2], w0_words, 4, 8, c0, c1)
 

@@ -262,7 +262,7 @@ def tile_multiheadselfattention_pa_kernel(
         last = (len(blocks) - 1, TOK_TILES - 1)
         for b in range(1, len(blocks)):
             for t in range(TOK_TILES):
-                cuts = [0, NB // 2, NB] if (b, t) == last else [0, NB]
+                cuts = [0, NB // 2, 3 * NB // 4, NB] if (b, t) == last else [0, NB]
                 for n0, n1 in zip(cuts[:-1], cuts[1:]):
                     acc = psum.tile([P, n1 - n0], F32, name="acc")
                     for g in range(PASSES):

@@ -20,7 +20,7 @@ NB = 512
 HEADS = NB // HD
 HALF = HD // 2
 TWO_PI = 6.283185307179586
-WARM_FREE = 4
+WARM_FREE = 8
 WARM_HELD = 6
 
 

from contextlib import ExitStack

import concourse.mybir as mybir

T, E, HD = 1024, 4096, 128
FLOPS = 2 * T * E * 4096

F32 = mybir.dt.float32
I32 = mybir.dt.int32
BF16 = mybir.dt.bfloat16
U8 = mybir.dt.uint8
FP4X4 = mybir.dt.float4_e2m1fn_x4
ALU = mybir.AluOpType
ACT = mybir.ActivationFunctionType

P = 128
PASSES = E // 512
TOK_TILES = T // P
NB = 512
HEADS = NB // HD
HALF = HD // 2
TWO_PI = 6.283185307179586
WARM_FREE = 8
WARM_HELD = 6


def load_codes(nc, tile, words, g0, g1, c0, c1):
    nc.sync.dma_start(
        out=tile[:].bitcast(I32),
        in_=words[g0:g1, :, 2 * c0 : 2 * c1].rearrange("g p n -> p g n").bitcast(I32),
    )


def load_scales(nc, tile, scales, g0, g1, c0, c1, rows=(0, 1, 2, 3)):
    for r in rows:
        nc.sync.dma_start(
            out=tile[r : P : 32, :, :].bitcast(I32),
            in_=scales[g0:g1, r : 16 : 4, c0:c1].rearrange("g q n -> q g n").bitcast(I32),
        )


def tile_multiheadselfattention_pa_kernel(
    tc, x_words, x_scales, wq_words, wq_scales, wk_words, wk_scales, wv_words, wv_scales, out_q, out_k, out_v
):
    nc = tc.nc
    outs = {
        "q": out_q.rearrange("b t h d -> (b t) (h d)"),
        "k": out_k.rearrange("b t h d -> (b t) (h d)"),
        "v": out_v.rearrange("b t h d -> (b t) (h d)"),
    }
    weights = {"q": (wq_words, wq_scales), "k": (wk_words, wk_scales), "v": (wv_words, wv_scales)}
    blocks = [("v", 0), ("q", 0), ("q", 1), ("q", 2), ("q", 3), ("k", 0), ("k", 1), ("v", 1)]
    code_runs = [(0, 1), (1, 4), (4, 8)]
    x_scale_runs = [(0, 2), (2, 8)]
    w_scale_runs = [(0, 8)]

    with ExitStack() as ctx:
        ctx.enter_context(tc.manual_schedule())
        keep = ctx.enter_context(tc.tile_pool(name="keep", bufs=1))
        stage = ctx.enter_context(tc.tile_pool(name="stage", bufs=1))
        psum = ctx.enter_context(tc.psum_pool(name="psum", bufs=8))

        warm = keep.tile([P, NB], BF16, name="warm")
        nc.gpsimd.memset(warm[:], 0.0)

        pos_i = keep.tile([P, TOK_TILES], I32, name="pos_i")
        nc.gpsimd.iota(pos_i[:], pattern=[[P, TOK_TILES]], base=0, channel_multiplier=1)
        idx_i = keep.tile([P, HALF], I32, name="idx_i")
        nc.gpsimd.iota(idx_i[:], pattern=[[1, HALF]], base=0, channel_multiplier=0)

        x_code, x_scale = [], []
        w_code = [[] for b in blocks]
        w_scale = [[] for b in blocks]

        xc_tiles, wc_tiles, xs_tiles, ws_tiles = [], [], [], []
        for r, (g0, g1) in enumerate(code_runs):
            xc = keep.tile([P, g1 - g0, 2 * T], U8, name="xc%d" % r, align_bytes=256)
            wc = keep.tile([P, g1 - g0, 2 * NB], U8, name="wc0_%d" % r, align_bytes=256)
            xc_tiles.append(xc)
            wc_tiles.append(wc)
            for g in range(g0, g1):
                x_code.append((xc, g - g0))
                w_code[0].append((wc, g - g0))
        for r, (g0, g1) in enumerate(x_scale_runs):
            xs = keep.tile([P, g1 - g0, T], U8, name="xs%d" % r, align_bytes=256)
            xs_tiles.append(xs)
            for g in range(g0, g1):
                x_scale.append((xs, g - g0))
        for r, (g0, g1) in enumerate(w_scale_runs):
            ws = keep.tile([P, g1 - g0, NB], U8, name="ws0_%d" % r, align_bytes=256)
            ws_tiles.append(ws)
            for g in range(g0, g1):
                w_scale[0].append((ws, g - g0))

        kind0, col0 = blocks[0]
        w0_words, w0_scales = weights[kind0]
        c0, c1 = col0 * NB, (col0 + 1) * NB

        nc.vector.memset(xs_tiles[0][:].bitcast(I32), 0)
        nc.vector.memset(ws_tiles[0][:].bitcast(I32), 0)
        warm_acc = psum.tile([P, NB], F32, name="acc")
        for i in range(WARM_FREE):
            nc.tensor.matmul(out=warm_acc[:], lhsT=warm[:, 0:P], rhs=warm[:], start=True, stop=True)
        load_codes(nc, xc_tiles[0], x_words, 0, 1, 0, T)
        load_codes(nc, wc_tiles[0], w0_words, 0, 1, c0, c1)
        gate = keep.tile([P, 4], U8, name="gate")
        nc.gpsimd.tensor_copy(out=gate[:], in_=wc_tiles[0][:, 0, 0:4])
        held = keep.tile([P, P], BF16, name="held")
        nc.gpsimd.memset(held[:], 0.0)
        for i in range(WARM_HELD):
            nc.tensor.matmul(out=warm_acc[:], lhsT=held[:], rhs=warm[:], start=True, stop=True)
        load_scales(nc, xs_tiles[0], x_scales, 0, 2, 0, T, rows=(0, 1))
        load_scales(nc, ws_tiles[0], w0_scales, 0, 8, c0, c1)
        load_scales(nc, xs_tiles[0], x_scales, 0, 2, 0, T, rows=(2, 3))
        nc.vector.memset(xs_tiles[1][:].bitcast(I32), 0)
        load_codes(nc, xc_tiles[1], x_words, 1, 4, 0, T)
        load_codes(nc, wc_tiles[1], w0_words, 1, 4, c0, c1)
        load_scales(nc, xs_tiles[1], x_scales, 2, 8, 0, T)
        load_codes(nc, xc_tiles[2], x_words, 4, 8, 0, T)
        load_codes(nc, wc_tiles[2], w0_words, 4, 8, c0, c1)

        late_planes = []
        for b in range(1, len(blocks)):
            wc = keep.tile([P, PASSES, 2 * NB], U8, name="wc%d" % b, align_bytes=256)
            ws = keep.tile([P, PASSES, NB], U8, name="ws%d" % b, align_bytes=256)
            late_planes.append((b, wc, ws))
            for g in range(PASSES):
                w_code[b].append((wc, g))
                w_scale[b].append((ws, g))

        def load_block(b, wc, ws):
            kind, col = blocks[b]
            words, scales = weights[kind]
            nc.vector.memset(ws[:].bitcast(I32), 0)
            load_codes(nc, wc, words, 0, PASSES, col * NB, (col + 1) * NB)
            load_scales(nc, ws, scales, 0, PASSES, col * NB, (col + 1) * NB)

        for b, wc, ws in late_planes[:2]:
            load_block(b, wc, ws)

        posf = keep.tile([P, TOK_TILES], F32, name="posf")
        nc.vector.tensor_copy(out=posf[:], in_=pos_i[:])
        idxf = keep.tile([P, HALF], F32, name="idxf")
        nc.vector.tensor_copy(out=idxf[:], in_=idx_i[:])
        base = keep.tile([P, HALF], F32, name="base")
        nc.vector.tensor_scalar(
            out=base[:], in0=idxf[:], scalar1=2.0 / (1.4 * HD), scalar2=0.4 / 1.4, op0=ALU.mult, op1=ALU.add
        )
        lnb = keep.tile([P, HALF], F32, name="lnb")
        nc.scalar.activation(out=lnb[:], in_=base[:], func=ACT.Ln)
        power = keep.tile([P, TOK_TILES], F32, name="power")
        nc.vector.tensor_scalar(
            out=power[:], in0=posf[:], scalar1=-512.0, scalar2=1.0 / 512.0, op0=ALU.add, op1=ALU.mult
        )
        turns = keep.tile([P, HALF], F32, name="turns")
        nc.vector.tensor_scalar(
            out=turns[:, 0:1], in0=posf[:, 0:1], scalar1=0.0, scalar2=1.0 / TWO_PI, op0=ALU.mult, op1=ALU.add
        )
        n = 1
        while n < HALF:
            nc.vector.tensor_scalar(
                out=turns[:, n : 2 * n], in0=turns[:, 0:n], scalar1=10000.0 ** (-n / float(HALF)), scalar2=None, op0=ALU.mult
            )
            n *= 2
        shape3 = [P, TOK_TILES, HALF]
        ang = keep.tile([P, TOK_TILES, 2, HALF], F32, name="ang")
        nc.vector.tensor_tensor(
            out=ang[:, :, 0, :],
            in0=turns[:].unsqueeze(1).to_broadcast(shape3),
            in1=posf[:].unsqueeze(2).to_broadcast(shape3),
            op=ALU.mult,
        )
        expo = keep.tile(shape3, F32, name="expo")
        nc.vector.tensor_tensor(
            out=expo[:],
            in0=lnb[:].unsqueeze(1).to_broadcast(shape3),
            in1=power[:].unsqueeze(2).to_broadcast(shape3),
            op=ALU.mult,
        )
        decay = keep.tile([P, 2, TOK_TILES, HALF], F32, name="decay")
        nc.scalar.activation(out=decay[:, 0], in_=expo[:], func=ACT.Exp)
        nc.scalar.activation(out=decay[:, 1], in_=expo[:], func=ACT.Exp, scale=-1.0)
        nc.vector.tensor_scalar(out=ang[:, :, 1, :], in0=ang[:, :, 0, :], scalar1=0.25, scalar2=None, op0=ALU.add)
        whole = keep.tile([P, TOK_TILES, 2, HALF], I32, name="whole")
        nc.vector.tensor_copy(out=whole[:], in_=ang[:])
        nc.vector.tensor_tensor(out=ang[:], in0=ang[:], in1=whole[:], op=ALU.subtract)
        nc.vector.scalar_tensor_tensor(out=ang[:], in0=ang[:], scalar=0.5, in1=ang[:], op0=ALU.is_gt, op1=ALU.subtract)
        sincos = keep.tile([P, TOK_TILES, 2, HALF], F32, name="sincos")
        nc.scalar.activation(out=sincos[:], in_=ang[:], func=ACT.Sin, scale=-TWO_PI)

        cos_tab, sin_tab = {}, {}
        for j, kind in enumerate(("q", "k")):
            ct = keep.tile([P, TOK_TILES, 2, HALF], F32, name="cos_" + kind)
            st = keep.tile([P, TOK_TILES, 2, HALF], F32, name="sin_" + kind)
            for two in range(2):
                nc.vector.tensor_tensor(out=ct[:, :, two, :], in0=sincos[:, :, 1, :], in1=decay[:, j], op=ALU.mult)
            nc.vector.tensor_tensor(out=st[:, :, 0, :], in0=sincos[:, :, 0, :], in1=decay[:, j], op=ALU.mult)
            nc.vector.scalar_tensor_tensor(
                out=st[:, :, 1, :], in0=sincos[:, :, 0, :], scalar=-1.0, in1=decay[:, j], op0=ALU.mult, op1=ALU.mult
            )
            cos_tab[kind] = ct
            sin_tab[kind] = st

        for b, wc, ws in late_planes[2:]:
            load_block(b, wc, ws)

        def mx_pass(acc, b, t, g, n0=0, n1=NB):
            xc, xi = x_code[g]
            xs, si = x_scale[g]
            wc, wi = w_code[b][g]
            ws, wj = w_scale[b][g]
            nc.tensor.matmul_mx(
                out=acc[:],
                lhsT=xc[:, xi, 2 * P * t : 2 * P * (t + 1)].bitcast(FP4X4),
                lhsT_scale=xs[:, si, P * t : P * (t + 1)],
                rhs=wc[:, wi, 2 * n0 : 2 * n1].bitcast(FP4X4),
                rhs_scale=ws[:, wj, n0:n1],
                start=(g == 0),
                stop=(g == PASSES - 1),
            )

        def finish(acc, b, t, n0=0, n1=NB):
            kind, col = blocks[b]
            dst = outs[kind][P * t : P * (t + 1), col * NB + n0 : col * NB + n1]
            if kind == "v":
                vo = stage.tile([P, n1 - n0], F32, name="vo", bufs=10)
                nc.scalar.copy(out=vo[:], in_=acc[:])
                nc.sync.dma_start(out=dst, in_=vo[:])
                return
            shape_h = [P, HEADS, HD]
            acc_h = acc[:].rearrange("p (h d) -> p h d", h=HEADS)
            direct = stage.tile([P, HEADS, 2, HALF], F32, name="direct", bufs=6)
            cross = stage.tile([P, HEADS, 2, HALF], F32, name="cross", bufs=4)
            nc.vector.tensor_tensor(
                out=direct[:].rearrange("p h two i -> p h (two i)"),
                in0=acc_h,
                in1=cos_tab[kind][:, t].rearrange("p two i -> p (two i)").unsqueeze(1).to_broadcast(shape_h),
                op=ALU.mult,
            )
            nc.vector.tensor_tensor(
                out=cross[:].rearrange("p h two i -> p h (two i)"),
                in0=acc_h,
                in1=sin_tab[kind][:, t].rearrange("p two i -> p (two i)").unsqueeze(1).to_broadcast(shape_h),
                op=ALU.mult,
            )
            for two in range(2):
                nc.vector.tensor_tensor(
                    out=direct[:, :, two, :], in0=direct[:, :, two, :], in1=cross[:, :, 1 - two, :], op=ALU.add
                )
            nc.sync.dma_start(out=dst, in_=direct[:].rearrange("p h two i -> p (h two i)"))

        accs = []
        for t in range(TOK_TILES):
            acc0 = psum.tile([P, NB], F32, name="acc")
            accs.append(acc0)
        for g in range(PASSES):
            for t in range(TOK_TILES):
                mx_pass(accs[t], 0, t, g)
        for t in range(TOK_TILES):
            finish(accs[t], 0, t)

        last = (len(blocks) - 1, TOK_TILES - 1)
        for b in range(1, len(blocks)):
            for t in range(TOK_TILES):
                cuts = [0, NB // 2, 3 * NB // 4, NB] if (b, t) == last else [0, NB]
                for n0, n1 in zip(cuts[:-1], cuts[1:]):
                    acc = psum.tile([P, n1 - n0], F32, name="acc")
                    for g in range(PASSES):
                        mx_pass(acc, b, t, g, n0, n1)
                    finish(acc, b, t, n0, n1)
